import numpy as np
import ml_dtypes


def mxq(x, axis, fmt="e4m3"):
    dtype, down = {"e4m3": (ml_dtypes.float8_e4m3fn, 7), "e5m2": (ml_dtypes.float8_e5m2, 14)}[fmt]
    v = np.moveaxis(np.asarray(x, np.float32).astype(ml_dtypes.bfloat16).astype(np.float64), axis, -1)
    blocks = v.reshape(v.shape[:-1] + (-1, 32))
    amax = np.abs(blocks).max(-1, keepdims=True)
    byte = np.maximum(np.where(amax > 0, np.frexp(amax)[1] - 1 + 127, 0) - down, 1)
    scale = np.exp2(byte - 127.0)
    codes = (blocks / scale).astype(np.float32).astype(dtype).astype(np.float64)
    return np.moveaxis((codes * scale).reshape(v.shape), -1, axis)


WIDE = False


def mx_kscale(k):
    if not WIDE:
        return np.ones(k)
    levels = np.array([10, -10, 5, -5, 0])
    if k % 512:
        return np.exp2(np.random.permutation(np.resize(levels, k // 32))).repeat(32)
    a = np.empty((k // 512, 16))
    for p in range(k // 512):
        a[p, :8] = np.random.permutation(np.resize(levels, 8))
        for g in range(8):
            far = levels[np.abs(levels - a[p, g]) >= 10]
            a[p, g + 8] = far[np.random.randint(len(far))]
    return np.exp2(a.ravel()).repeat(32)


BF16 = ml_dtypes.bfloat16


def bf(x):
    return np.asarray(x, np.float32).astype(BF16)


def f64(x):
    return np.asarray(x).astype(np.float64)


B, DIN, H1, H2, N, I, K, O = 4096, 2048, 1024, 1024, 32, 8, 256, 16
NI = N * I
LN_EPS = 1e-5


def draw0():
    s, t = mx_kscale(H1), mx_kscale(H2)
    return {"h1": bf(np.maximum(np.random.standard_normal((B, H1)), 0.0) * s),
            "W2": bf(np.random.standard_normal((H1, H2)) * 1.4 / np.sqrt(H1) / s[:, None] * t),
            "b2": bf(np.random.standard_normal(H2) * 0.2 * t),
            "Wp": bf(np.random.standard_normal((N, H2, I)) * 1.4 / np.sqrt(H2) / t[None, :, None]),
            "bp": bf(np.random.standard_normal((N, I)) * 0.2),
            "ln_g": bf(1.0 + 0.1 * np.random.standard_normal((N, I))),
            "ln_b": bf(0.1 * np.random.standard_normal((N, I)))}


def core(h1, W2, b2, Wp, bp, ln_g, ln_b):
    x = np.maximum((mxq(f64(h1), 1, "e4m3") @ mxq(f64(W2), 0, "e4m3")) + f64(b2), 0.0)
    wpf = f64(Wp).transpose(1, 0, 2).reshape(H2, NI)
    p = (mxq(x, 1, "e4m3") @ mxq(wpf, 0, "e4m3")).reshape(B, N, I) + f64(bp)
    mu = p.mean(-1, keepdims=True)
    var = ((p - mu) ** 2).mean(-1, keepdims=True)
    return (p - mu) / np.sqrt(var + LN_EPS) * f64(ln_g) + f64(ln_b)


def e4m3fn_bytes(y):
    return np.clip(np.asarray(y, np.float64), -448.0, 448.0).astype(np.float32).astype(ml_dtypes.float8_e4m3fn).view(np.uint8)


def e4m3fn_values(b):
    return np.asarray(b, np.uint8).view(ml_dtypes.float8_e4m3fn).astype(np.float64)


def setup_inputs():
    d = draw0()
    x0 = np.asarray(d['h1']).astype(np.float64)
    s = (np.max(np.abs(x0), axis=(0,), keepdims=True) / 448.0).astype(np.float32)
    out = {}
    for k, v in d.items():
        if k == 'h1':
            out['h1_bytes'] = e4m3fn_bytes(x0 / s.astype(np.float64))
            out['h1_scale'] = s
        else:
            out[k] = v
    return out


def reference(h1_bytes, h1_scale, W2, b2, Wp, bp, ln_g, ln_b):
    return core(e4m3fn_values(h1_bytes) * h1_scale.astype(np.float64), W2, b2, Wp, bp, ln_g, ln_b)

@@ -1,0 +1,385 @@
+from contextlib import ExitStack
+
+import concourse.mybir as mybir
+from concourse.masks import make_identity
+
+F32 = mybir.dt.float32
+BF16 = mybir.dt.bfloat16
+U32 = mybir.dt.uint32
+U8 = mybir.dt.uint8
+FP8 = mybir.dt.float8_e4m3fn
+FP8X4 = mybir.dt.float8_e4m3fn_x4
+ALU = mybir.AluOpType
+ACT = mybir.ActivationFunctionType
+AXIS = mybir.AxisListType
+
+TOKENS, H1, H2, CAPS, DIM = 4096, 1024, 1024, 32, 8
+OUT = CAPS * DIM
+LN_EPS = 1e-5
+FLOPS = 2 * TOKENS * H1 * H2 + 2 * TOKENS * H2 * OUT
+
+P = 128
+PACK = 4
+K_PASS = P * PACK
+PASSES = H1 // K_PASS
+GROUP_ROWS = [4] * 8
+GROUPS = len(GROUP_ROWS)
+ON_TENSOR = range(6)
+SCALAR_SHARE = [0,0,384,384,384,384,384,256]
+
+
+def tile_capsulenetwork_pa_t_kernel(tc, h1_bytes, h1_scale, W2, b2, Wp, bp, ln_g, ln_b, out):
+    nc = tc.nc
+    first = [P * sum(GROUP_ROWS[:i]) for i in range(GROUPS + 1)]
+    out_rows = [out[first[i]:first[i + 1]].rearrange("(p j) n d -> p (j n d)", p=P) for i in range(GROUPS)]
+    h1_rows = [h1_bytes[first[i]:first[i + 1]].rearrange("(p j) k -> p (j k)", p=P) for i in range(GROUPS)]
+
+    with ExitStack() as ctx:
+        keep = ctx.enter_context(tc.tile_pool(name="keep", bufs=1))
+        work = ctx.enter_context(tc.tile_pool(name="work", bufs=2))
+        banks = ctx.enter_context(tc.psum_pool(name="banks", bufs=6))
+        centred_banks = ctx.enter_context(tc.psum_pool(name="centred_banks", bufs=2))
+        ctx.enter_context(tc.manual_schedule())
+
+        scale_cols = keep.tile([P, H1 // P], F32, name="scale_cols")
+        nc.sync.dma_start(out=scale_cols[:], in_=h1_scale.rearrange("o (p c) -> p (o c)", p=P))
+        w2_view = W2.rearrange("(g p j) (G c) -> G g p j c", p=P, j=PACK, c=K_PASS)
+        w2_raw = {}
+        h1_raw = {}
+
+        def load_w2(G, g):
+            w2_raw[G, g] = keep.tile([P, PACK, K_PASS], BF16, name="w2_raw%d%d" % (G, g))
+            nc.sync.dma_start(out=w2_raw[G, g][:], in_=w2_view[G, g])
+
+        def load_h1(i):
+            h1_raw[i] = keep.tile([P, GROUP_ROWS[i] * H1], U8, name="h1_raw%d" % i)
+            nc.sync.dma_start(out=h1_raw[i][:], in_=h1_rows[i])
+
+        load_w2(0, 0)
+        load_h1(0)
+        load_w2(0, 1)
+        load_w2(1, 0)
+        load_w2(1, 1)
+        load_h1(1)
+        b2_cols = keep.tile([P, PASSES, PACK], BF16, name="b2_cols")
+        nc.sync.dma_start(out=b2_cols[:], in_=b2.rearrange("(G p t) -> p G t", p=P, t=PACK))
+        load_h1(2)
+        wp_raw = {}
+        wp_view = Wp.rearrange("n (G p j) d -> G p n (j d)", p=P, j=PACK)
+        for G in range(PASSES):
+            wp_raw[G] = keep.tile([P, CAPS, PACK * DIM], BF16, name="wp_raw%d" % G)
+            nc.sync.dma_start(out=wp_raw[G][:], in_=wp_view[G])
+        bp_cols = keep.tile([P, 2, 2], BF16, name="bp_cols")
+        with nc.allow_non_contiguous_dma(reason="one bias value to a partition"):
+            nc.sync.dma_start(out=bp_cols[:, :, 0:1], in_=bp.rearrange("(h n) (d o) -> (n d) h o", h=2, o=1))
+        gain = keep.tile([P, OUT], BF16, name="gain")
+        nc.sync.dma_start(out=gain[:], in_=ln_g.rearrange("n d -> (n d)").partition_broadcast(P))
+        shift = keep.tile([P, OUT], BF16, name="shift")
+        nc.sync.dma_start(out=shift[:], in_=ln_b.rearrange("n d -> (n d)").partition_broadcast(P))
+        for i in range(3, GROUPS):
+            load_h1(i)
+
+        ident = keep.tile([P, P], F32, name="ident")
+        make_identity(nc, ident[:])
+        centre = keep.tile([P, P], F32, name="centre")
+        blocks = [[-DIM, P // DIM], [0, DIM]]
+        nc.gpsimd.memset(centre[:], 0.0)
+        nc.gpsimd.affine_select(out=centre[:], in_=centre[:], compare_op=ALU.is_gt, fill=-1.0 / DIM,
+                                base=1 - DIM, pattern=blocks, channel_multiplier=1)
+        nc.gpsimd.affine_select(out=centre[:], in_=centre[:], compare_op=ALU.is_ge, fill=0.0,
+                                base=0, pattern=blocks, channel_multiplier=1)
+        nc.gpsimd.affine_select(out=centre[:], in_=centre[:], compare_op=ALU.not_equal, fill=1.0 - 1.0 / DIM,
+                                base=0, pattern=[[-1, P]], channel_multiplier=1)
+
+        warm = keep.tile([P, 1], F32, name="warm")
+        nc.scalar.activation(out=warm[:], in_=ident[:, 0:1], func=ACT.Abs_reciprocal_sqrt, bias=LN_EPS, scale=1.0)
+
+        scale_all = keep.tile([P, H1], F32, name="scale_all")
+        per_bank = 4
+        for half in range(2):
+            bank = banks.tile([P, 512], F32, name="bank")
+            for c in range(per_bank):
+                col = half * per_bank + c
+                nc.tensor.transpose(bank[:, c * P:(c + 1) * P], scale_cols[:, col:col + 1].to_broadcast([P, P]), ident[:])
+            nc.scalar.copy(out=scale_all[:].rearrange("q (p c) -> q p c", c=H1 // P)[:, :, half * per_bank:(half + 1) * per_bank],
+                           in_=bank[:].rearrange("q (c p) -> q p c", c=per_bank))
+
+        w2_codes = keep.tile([P, PASSES, H2], U32, name="w2_codes", align_bytes=64)
+        w2_scales = keep.tile([P, PASSES, H2], U8, name="w2_scales", align_bytes=64)
+        wp_codes = keep.tile([P, PASSES, OUT], U32, name="wp_codes", align_bytes=64)
+        wp_scales = keep.tile([P, PASSES, OUT], U8, name="wp_scales", align_bytes=64)
+        w2_grouped = {}
+        wp_grouped = {}
+
+        def group_w2(G, g, copy):
+            w2_grouped[G, g] = keep.tile([P, K_PASS * PACK], BF16, name="w2_grouped%d%d" % (G, g), align_bytes=64)
+            copy(out=w2_grouped[G, g][:].rearrange("p (t m j) -> p m t j", t=PACK, j=PACK),
+                 in_=w2_raw[G, g][:].rearrange("p j (m t) -> p m t j", t=PACK))
+
+        def quantize_w2(G, g):
+            cols = slice(G * K_PASS, (G + 1) * K_PASS)
+            nc.vector.quantize_mx(out=w2_codes[:, g, cols].bitcast(FP8X4), scales=w2_scales[:, g, cols], in_=w2_grouped[G, g][:])
+
+        def group_wp(G):
+            wp_grouped[G] = keep.tile([P, OUT * PACK], BF16, name="wp_grouped%d" % G, align_bytes=64)
+            nc.scalar.copy(out=wp_grouped[G][:].rearrange("p (n d j) -> p n d j", d=DIM, j=PACK),
+                           in_=wp_raw[G][:].rearrange("p n (j d) -> p n d j", j=PACK))
+
+        def quantize_wp(G):
+            nc.vector.quantize_mx(out=wp_codes[:, G, :].bitcast(FP8X4), scales=wp_scales[:, G, :], in_=wp_grouped[G][:])
+
+        h1_wide, h1_grouped, h1_codes, h1_scales = {}, {}, {}, {}
+        x_planes, x_grouped, x_codes, x_scales = {}, {}, {}, {}
+        u_cols, centred, squares, sums, rstd, result = {}, {}, {}, {}, {}, {}
+
+        sum_bank = {}
+
+        def valid(i):
+            return 0 <= i < GROUPS
+
+        def pairs(i):
+            rows = GROUP_ROWS[i] if valid(i) else 0
+            return [range(lo, min(lo + 2, rows)) for lo in range(0, rows, 2)]
+
+        def widen(i, pair):
+            if pair >= len(pairs(i)):
+                return
+            for j in pairs(i)[pair]:
+                h1_wide[i, j] = work.tile([P, H1], BF16, name="h1_wide", bufs=12, align_bytes=64)
+                nc.vector.tensor_tensor(out=h1_wide[i, j][:], in0=h1_raw[i][:, j * H1:(j + 1) * H1].bitcast(FP8),
+                                        in1=scale_all[:], op=ALU.mult)
+
+        def turn(i, pair):
+            for rows in pairs(i)[pair:pair + 1]:
+                width = len(rows) * P
+                for g in range(PASSES):
+                    if pair == 0:
+                        h1_grouped[i, g] = work.tile([P, GROUP_ROWS[i] * P * PACK], BF16, name="h1_grouped", bufs=4, align_bytes=64)
+                    words_out = h1_grouped[i, g][:].bitcast(F32).rearrange("p (n u) -> p n u", u=2)
+                    bank = banks.tile([P, 512], F32, name="bank")
+                    for u in range(2):
+                        for jj, j in enumerate(rows):
+                            words = h1_wide[i, j][:].bitcast(F32)
+                            col = u * width + jj * P
+                            nc.tensor.transpose(bank[:, col:col + P], words[:, 256 * g + u:256 * (g + 1):2], ident[:])
+                    nc.scalar.copy(out=words_out[:, 256 * pair:256 * pair + width, :],
+                                   in_=bank[:, 0:2 * width].rearrange("p (u n) -> p n u", u=2))
+
+        def quantize_h1(i, g):
+            if not valid(i):
+                return
+            n = GROUP_ROWS[i] * P
+            h1_codes[i, g] = work.tile([P, n], U32, name="h1_codes", bufs=4, align_bytes=64)
+            h1_scales[i, g] = work.tile([P, n], U8, name="h1_scales", bufs=4, align_bytes=64)
+            nc.vector.quantize_mx(out=h1_codes[i, g][:].bitcast(FP8X4), scales=h1_scales[i, g][:], in_=h1_grouped[i, g][:])
+
+        def hidden(i, G, planes):
+            if not valid(i):
+                return
+            n = GROUP_ROWS[i] * P
+            for t in planes:
+                if t == 0:
+                    x_planes[i, G] = work.tile([P, PACK, n], BF16, name="x_planes", bufs=4)
+                bank = banks.tile([P, 512], F32, name="bank")
+                cols = slice((G * PACK + t) * P, (G * PACK + t + 1) * P)
+                for g in range(PASSES):
+                    nc.tensor.matmul_mx(out=bank[:, 0:n], lhsT=w2_codes[:, g, cols].bitcast(FP8X4), lhsT_scale=w2_scales[:, g, cols],
+                                        rhs=h1_codes[i, g][:].bitcast(FP8X4), rhs_scale=h1_scales[i, g][:],
+                                        start=(g == 0), stop=(g == PASSES - 1))
+                nc.scalar.activation(out=x_planes[i, G][:, t, :], in_=bank[:, 0:n], func=ACT.Relu, bias=b2_cols[:, G, t:t + 1], scale=1.0)
+
+        def group_x(i, G, lo, hi, copy):
+            if not valid(i) or lo >= hi:
+                return
+            if (i, G) not in x_grouped:
+                x_grouped[i, G] = work.tile([P, GROUP_ROWS[i] * P * PACK], BF16, name="x_grouped", bufs=4, align_bytes=64)
+            dst = x_grouped[i, G][:].rearrange("p (c n t) -> p c t n", n=4, t=PACK)
+            src = x_planes[i, G][:].rearrange("p t (c n) -> p c t n", n=4)
+            copy(out=dst[:, lo // 4:hi // 4], in_=src[:, lo // 4:hi // 4])
+
+        def quantize_x(i, G):
+            if not valid(i):
+                return
+            n = GROUP_ROWS[i] * P
+            x_codes[i, G] = work.tile([P, n], U32, name="x_codes", bufs=4, align_bytes=64)
+            x_scales[i, G] = work.tile([P, n], U8, name="x_scales", bufs=4, align_bytes=64)
+            nc.vector.quantize_mx(out=x_codes[i, G][:].bitcast(FP8X4), scales=x_scales[i, G][:], in_=x_grouped[i, G][:])
+
+        def capsules(i):
+            if not valid(i):
+                return
+            n = GROUP_ROWS[i] * P
+            for h in range(2):
+                bank = banks.tile([P, 512], F32, name="bank")
+                cols = slice(h * P, (h + 1) * P)
+                for G in range(PASSES):
+                    nc.tensor.matmul_mx(out=bank[:, 0:n], lhsT=wp_codes[:, G, cols].bitcast(FP8X4), lhsT_scale=wp_scales[:, G, cols],
+                                        rhs=x_codes[i, G][:].bitcast(FP8X4), rhs_scale=x_scales[i, G][:],
+                                        start=(G == 0), stop=(G == PASSES - 1))
+                u_cols[i, h] = work.tile([P, n], F32, name="u_cols", bufs=4)
+                nc.scalar.activation(out=u_cols[i, h][:], in_=bank[:, 0:n], func=ACT.Identity, bias=bp_cols[:, h, 0:1], scale=1.0)
+
+        def subtract_mean(i):
+            for pair, rows in enumerate(pairs(i)):
+                if i == GROUPS - 1:
+                    centred[i, pair] = banks.tile([P, 512], F32, name="bank")
+                else:
+                    centred[i, pair] = centred_banks.tile([P, 512], F32, name="centred")
+                for jj, j in enumerate(rows):
+                    for h in range(2):
+                        col = jj * OUT + h * P
+                        nc.tensor.matmul(centred[i, pair][:, col:col + P], lhsT=u_cols[i, h][:, j * P:(j + 1) * P], rhs=centre[:],
+                                         start=True, stop=True)
+
+        def square(i, pair):
+            if pair >= len(pairs(i)):
+                return
+            if pair == 0:
+                squares[i] = work.tile([P, GROUP_ROWS[i] * OUT], F32, name="squares")
+            width = len(pairs(i)[pair]) * OUT
+            if i in ON_TENSOR:
+                nc.scalar.activation(out=squares[i][:].rearrange("p (d c) -> p d c", d=DIM)[:, :, 64 * pair:64 * (pair + 1)],
+                                     in_=centred[i, pair][:].rearrange("p (c d) -> p d c", d=DIM), func=ACT.Square)
+            else:
+                nc.scalar.activation(out=squares[i][:, 512 * pair:512 * pair + width], in_=centred[i, pair][:, 0:width], func=ACT.Square)
+
+        def add_squares(i):
+            if i not in ON_TENSOR:
+                return
+            sum_bank[i] = banks.tile([P, 512], F32, name="bank")
+            for d in range(DIM):
+                nc.tensor.matmul(sum_bank[i][:, 0:P], lhsT=squares[i][:, d * P:(d + 1) * P], rhs=ident[:],
+                                 start=(d == 0), stop=(d == DIM - 1), is_transpose=True)
+            sums[i] = work.tile([P, P], F32, name="sums")
+            nc.scalar.copy(out=sums[i][:], in_=sum_bank[i][:, 0:P])
+
+        def turn_sums_back(i):
+            if i not in ON_TENSOR:
+                return
+            bank = banks.tile([P, 512], F32, name="bank")
+            nc.tensor.transpose(bank[:, 0:P], sums[i][:], ident[:])
+            rstd[i] = work.tile([P, P], F32, name="rstd")
+            nc.scalar.activation(out=rstd[i][:], in_=bank[:, 0:P], func=ACT.Abs_reciprocal_sqrt, bias=LN_EPS, scale=1.0 / DIM)
+
+        def sum_squares(i, lo=0, hi=None):
+            if not valid(i) or i in ON_TENSOR:
+                return
+            hi = GROUP_ROWS[i] if hi is None else hi
+            if lo == 0:
+                sums[i] = work.tile([P, GROUP_ROWS[i] * CAPS], F32, name="sums")
+            nc.vector.tensor_reduce(out=sums[i][:, lo * CAPS:hi * CAPS],
+                                    in_=squares[i][:, lo * OUT:hi * OUT].rearrange("p (n d) -> p n d", d=DIM), axis=AXIS.X, op=ALU.add)
+
+        def inverse_root(i, lo=0, hi=None):
+            if not valid(i) or i in ON_TENSOR:
+                return
+            hi = GROUP_ROWS[i] if hi is None else hi
+            if lo == 0:
+                rstd[i] = work.tile([P, GROUP_ROWS[i] * CAPS], F32, name="rstd")
+            nc.scalar.activation(out=rstd[i][:, lo * CAPS:hi * CAPS], in_=sums[i][:, lo * CAPS:hi * CAPS],
+                                 func=ACT.Abs_reciprocal_sqrt, bias=LN_EPS, scale=1.0 / DIM)
+
+        def normalise(i, pair):
+            for rows in pairs(i)[pair:pair + 1]:
+                if pair == 0:
+                    result[i] = work.tile([P, GROUP_ROWS[i] * OUT], F32, name="result", bufs=3)
+                caps = len(rows) * CAPS
+                nc.vector.tensor_tensor(out=result[i][:, 512 * pair:512 * pair + caps * DIM].rearrange("p (n d) -> p n d", d=DIM),
+                                        in0=centred[i, pair][:, 0:caps * DIM].rearrange("p (n d) -> p n d", d=DIM),
+                                        in1=rstd[i][:, 64 * pair:64 * pair + caps].unsqueeze(2).to_broadcast([P, caps, DIM]),
+                                        op=ALU.mult)
+
+        def affine(i, vector, op, engine, lo=0, hi=None):
+            if not valid(i):
+                return
+            hi = GROUP_ROWS[i] if hi is None else hi
+            rows = result[i][:].rearrange("p (j c) -> p j c", c=OUT)[:, lo:hi, :]
+            engine.tensor_tensor(out=rows, in0=rows, in1=vector[:].unsqueeze(1).to_broadcast([P, hi - lo, OUT]), op=op)
+
+        def store(i, lo=0, hi=None):
+            if not valid(i):
+                return
+            hi = GROUP_ROWS[i] if hi is None else hi
+            nc.sync.dma_start(out=out_rows[i][:, lo * OUT:hi * OUT], in_=result[i][:, lo * OUT:hi * OUT])
+
+        group_w2(0, 0, nc.vector.tensor_copy)
+        widen(0, 0)
+        group_w2(0, 1, nc.scalar.copy)
+        quantize_w2(0, 0)
+        widen(0, 1)
+        turn(0, 0)
+        turn(0, 1)
+        quantize_w2(0, 1)
+        group_w2(1, 0, nc.vector.tensor_copy)
+        group_w2(1, 1, nc.scalar.copy)
+        quantize_h1(0, 0)
+        quantize_h1(0, 1)
+        quantize_w2(1, 0)
+        widen(1, 0)
+        quantize_w2(1, 1)
+        last = GROUPS - 1
+        for k in range(GROUPS):
+            tokens = GROUP_ROWS[k] * P
+            share = SCALAR_SHARE[k]
+            sum_squares(k - 2)
+            quantize_x(k - 1, 1)
+            hidden(k, 0, range(0, 2))
+            inverse_root(k - 2)
+            hidden(k, 0, range(2, 4))
+            widen(k + 1, 1)
+            hidden(k, 1, range(0, 2))
+            add_squares(k - 2)
+            hidden(k, 1, range(2, 4))
+            turn_sums_back(k - 2)
+            if k == 1:
+                quantize_wp(0)
+                quantize_wp(1)
+            capsules(k - 1)
+            group_x(k, 0, 0, tokens, nc.vector.tensor_copy)
+            normalise(k - 2, 0)
+            normalise(k - 2, 1)
+            turn(k + 1, 0)
+            turn(k + 1, 1)
+            if k == 0:
+                group_wp(0)
+                group_wp(1)
+            group_x(k, 1, share, tokens, nc.vector.tensor_copy)
+            quantize_x(k, 0)
+            if k == last:
+                group_x(k, 1, 0, share, nc.scalar.copy)
+                quantize_x(k, 1)
+                share = 0
+            affine(k - 2, gain, ALU.mult, nc.vector)
+            quantize_h1(k + 1, 0)
+            quantize_h1(k + 1, 1)
+            subtract_mean(k - 1)
+            group_x(k, 1, 0, share // 2, nc.scalar.copy)
+            square(k - 1, 0)
+            group_x(k, 1, share // 2, share, nc.scalar.copy)
+            square(k - 1, 1)
+            affine(k - 2, shift, ALU.add, nc.vector)
+            store(k - 2)
+            widen(k + 2, 0)
+        capsules(last)
+        sum_squares(last - 1)
+        inverse_root(last - 1)
+        subtract_mean(last)
+        normalise(last - 1, 0)
+        normalise(last - 1, 1)
+        steps = [(2 * q, 2 * q + len(rows)) for q, rows in enumerate(pairs(last))]
+        for q in range(len(steps)):
+            square(last, q)
+        affine(last - 1, gain, ALU.mult, nc.vector)
+        for q, (lo, hi) in enumerate(steps):
+            sum_squares(last, lo, hi)
+            inverse_root(last, lo, hi)
+            if q == 0:
+                affine(last - 1, shift, ALU.add, nc.vector)
+                store(last - 1)
+        for q in range(len(steps)):
+            normalise(last, q)
+        for lo, hi in steps:
+            affine(last, gain, ALU.mult, nc.vector, lo, hi)
+        for lo, hi in steps:
+            affine(last, shift, ALU.add, nc.vector, lo, hi)
+            store(last, lo, hi)

@@ -24,8 +24,8 @@ K_PASS = P * PACK
 PASSES = H1 // K_PASS
 GROUP_ROWS = [4] * 8
 GROUPS = len(GROUP_ROWS)
-ON_TENSOR = range(6)
-SCALAR_SHARE = [0,0,384,384,384,384,384,256]
+ON_TENSOR = range(5)
+SCALAR_SHARE = [0,0,384,384,384,384,0,128]
 
 
 def tile_capsulenetwork_pa_t_kernel(tc, h1_bytes, h1_scale, W2, b2, Wp, bp, ln_g, ln_b, out):
@@ -133,6 +133,7 @@ def tile_capsulenetwork_pa_t_kernel(tc, h1_bytes, h1_scale, W2, b2, Wp, bp, ln_g
         u_cols, centred, squares, sums, rstd, result = {}, {}, {}, {}, {}, {}
 
         sum_bank = {}
+        capsule_bank = {}
 
         def valid(i):
             return 0 <= i < GROUPS
@@ -205,31 +206,43 @@ def tile_capsulenetwork_pa_t_kernel(tc, h1_bytes, h1_scale, W2, b2, Wp, bp, ln_g
             x_scales[i, G] = work.tile([P, n], U8, name="x_scales", bufs=4, align_bytes=64)
             nc.vector.quantize_mx(out=x_codes[i, G][:].bitcast(FP8X4), scales=x_scales[i, G][:], in_=x_grouped[i, G][:])
 
-        def capsules(i):
+        def capsules(i, passes=range(PASSES)):
             if not valid(i):
                 return
-            n = GROUP_ROWS[i] * P
             for h in range(2):
-                bank = banks.tile([P, 512], F32, name="bank")
                 cols = slice(h * P, (h + 1) * P)
-                for G in range(PASSES):
-                    nc.tensor.matmul_mx(out=bank[:, 0:n], lhsT=wp_codes[:, G, cols].bitcast(FP8X4), lhsT_scale=wp_scales[:, G, cols],
+                for G in passes:
+                    if G == 0:
+                        capsule_bank[i, h] = banks.tile([P, 512], F32, name="bank")
+                    nc.tensor.matmul_mx(out=capsule_bank[i, h][:], lhsT=wp_codes[:, G, cols].bitcast(FP8X4), lhsT_scale=wp_scales[:, G, cols],
                                         rhs=x_codes[i, G][:].bitcast(FP8X4), rhs_scale=x_scales[i, G][:],
                                         start=(G == 0), stop=(G == PASSES - 1))
-                u_cols[i, h] = work.tile([P, n], F32, name="u_cols", bufs=4)
-                nc.scalar.activation(out=u_cols[i, h][:], in_=bank[:, 0:n], func=ACT.Identity, bias=bp_cols[:, h, 0:1], scale=1.0)
+                if PASSES - 1 in passes:
+                    u_cols[i, h] = work.tile([P, 512], F32, name="u_cols", bufs=4)
+                    nc.scalar.activation(out=u_cols[i, h][:], in_=capsule_bank[i, h][:], func=ACT.Identity, bias=bp_cols[:, h, 0:1], scale=1.0)
 
-        def subtract_mean(i):
-            for pair, rows in enumerate(pairs(i)):
-                if i == GROUPS - 1:
-                    centred[i, pair] = banks.tile([P, 512], F32, name="bank")
-                else:
-                    centred[i, pair] = centred_banks.tile([P, 512], F32, name="centred")
+        def subtract_mean(i, which, matrices, pool, name):
+            for pair in (which if valid(i) else ()):
+                rows = pairs(i)[pair]
+                bank = pool.tile([P, 512], F32, name=name)
                 for jj, j in enumerate(rows):
                     for h in range(2):
                         col = jj * OUT + h * P
-                        nc.tensor.matmul(centred[i, pair][:, col:col + P], lhsT=u_cols[i, h][:, j * P:(j + 1) * P], rhs=centre[:],
+                        nc.tensor.matmul(bank[:, col:col + P], lhsT=u_cols[i, h][:, j * P:(j + 1) * P], rhs=matrices[h],
                                          start=True, stop=True)
+                centred[i, pair, name] = bank
+
+        centre_gain = keep.tile([P, 2, P], F32, name="centre_gain")
+
+        def fold_gain():
+            nc.vector.tensor_tensor(out=centre_gain[:], in0=centre[:].unsqueeze(1).to_broadcast([P, 2, P]),
+                                    in1=gain[:].rearrange("p (h c) -> p h c", h=2), op=ALU.mult)
+
+        def centre_plain(i):
+            subtract_mean(i, range(2), [centre[:], centre[:]], centred_banks, "centred")
+
+        def centre_gained(i, pair):
+            subtract_mean(i, [pair], [centre_gain[:, 0, :], centre_gain[:, 1, :]], banks, "bank")
 
         def square(i, pair):
             if pair >= len(pairs(i)):
@@ -239,9 +252,9 @@ def tile_capsulenetwork_pa_t_kernel(tc, h1_bytes, h1_scale, W2, b2, Wp, bp, ln_g
             width = len(pairs(i)[pair]) * OUT
             if i in ON_TENSOR:
                 nc.scalar.activation(out=squares[i][:].rearrange("p (d c) -> p d c", d=DIM)[:, :, 64 * pair:64 * (pair + 1)],
-                                     in_=centred[i, pair][:].rearrange("p (c d) -> p d c", d=DIM), func=ACT.Square)
+                                     in_=centred[i, pair, "centred"][:].rearrange("p (c d) -> p d c", d=DIM), func=ACT.Square)
             else:
-                nc.scalar.activation(out=squares[i][:, 512 * pair:512 * pair + width], in_=centred[i, pair][:, 0:width], func=ACT.Square)
+                nc.scalar.activation(out=squares[i][:, 512 * pair:512 * pair + width], in_=centred[i, pair, "centred"][:, 0:width], func=ACT.Square)
 
         def add_squares(i):
             if i not in ON_TENSOR:
@@ -285,7 +298,7 @@ def tile_capsulenetwork_pa_t_kernel(tc, h1_bytes, h1_scale, W2, b2, Wp, bp, ln_g
                     result[i] = work.tile([P, GROUP_ROWS[i] * OUT], F32, name="result", bufs=3)
                 caps = len(rows) * CAPS
                 nc.vector.tensor_tensor(out=result[i][:, 512 * pair:512 * pair + caps * DIM].rearrange("p (n d) -> p n d", d=DIM),
-                                        in0=centred[i, pair][:, 0:caps * DIM].rearrange("p (n d) -> p n d", d=DIM),
+                                        in0=centred[i, pair, "bank" if i >= GROUPS - 2 else "centred"][:, 0:caps * DIM].rearrange("p (n d) -> p n d", d=DIM),
                                         in1=rstd[i][:, 64 * pair:64 * pair + caps].unsqueeze(2).to_broadcast([P, caps, DIM]),
                                         op=ALU.mult)
 
@@ -318,24 +331,22 @@ def tile_capsulenetwork_pa_t_kernel(tc, h1_bytes, h1_scale, W2, b2, Wp, bp, ln_g
         widen(1, 0)
         quantize_w2(1, 1)
         last = GROUPS - 1
-        for k in range(GROUPS):
-            tokens = GROUP_ROWS[k] * P
+        for k in range(last):
             share = SCALAR_SHARE[k]
-            sum_squares(k - 2)
             quantize_x(k - 1, 1)
-            hidden(k, 0, range(0, 2))
-            inverse_root(k - 2)
-            hidden(k, 0, range(2, 4))
+            if k == 1:
+                quantize_wp(0)
+                quantize_wp(1)
+            hidden(k, 0, range(4))
             widen(k + 1, 1)
             hidden(k, 1, range(0, 2))
             add_squares(k - 2)
             hidden(k, 1, range(2, 4))
             turn_sums_back(k - 2)
-            if k == 1:
-                quantize_wp(0)
-                quantize_wp(1)
+            if k == 2:
+                fold_gain()
             capsules(k - 1)
-            group_x(k, 0, 0, tokens, nc.vector.tensor_copy)
+            group_x(k, 0, 0, 512, nc.vector.tensor_copy)
             normalise(k - 2, 0)
             normalise(k - 2, 1)
             turn(k + 1, 0)
@@ -343,16 +354,14 @@ def tile_capsulenetwork_pa_t_kernel(tc, h1_bytes, h1_scale, W2, b2, Wp, bp, ln_g
             if k == 0:
                 group_wp(0)
                 group_wp(1)
-            group_x(k, 1, share, tokens, nc.vector.tensor_copy)
+            group_x(k, 1, share, 512, nc.vector.tensor_copy)
             quantize_x(k, 0)
-            if k == last:
-                group_x(k, 1, 0, share, nc.scalar.copy)
-                quantize_x(k, 1)
-                share = 0
+            if k == last - 1:
+                break
             affine(k - 2, gain, ALU.mult, nc.vector)
             quantize_h1(k + 1, 0)
             quantize_h1(k + 1, 1)
-            subtract_mean(k - 1)
+            centre_plain(k - 1)
             group_x(k, 1, 0, share // 2, nc.scalar.copy)
             square(k - 1, 0)
             group_x(k, 1, share // 2, share, nc.scalar.copy)
@@ -360,26 +369,57 @@ def tile_capsulenetwork_pa_t_kernel(tc, h1_bytes, h1_scale, W2, b2, Wp, bp, ln_g
             affine(k - 2, shift, ALU.add, nc.vector)
             store(k - 2)
             widen(k + 2, 0)
-        capsules(last)
+        share = SCALAR_SHARE[last]
+        quantize_h1(last, 0)
+        quantize_h1(last, 1)
+        quantize_x(last - 1, 1)
+        centre_plain(last - 2)
+        square(last - 2, 0)
+        square(last - 2, 1)
+        affine(last - 3, gain, ALU.mult, nc.vector)
+        sum_squares(last - 2)
+        affine(last - 3, shift, ALU.add, nc.vector)
+        store(last - 3)
+        hidden(last, 0, range(4))
+        inverse_root(last - 2)
+        capsules(last - 1)
+        hidden(last, 1, range(4))
+        normalise(last - 2, 0)
+        normalise(last - 2, 1)
+        group_x(last, 0, 0, 512, nc.vector.tensor_copy)
+        affine(last - 2, gain, ALU.mult, nc.vector, 0, 2)
+        quantize_x(last, 0)
+        centre_plain(last - 1)
+        centre_gained(last - 1, 0)
+        capsules(last, range(1))
+        group_x(last, 1, 0, share, nc.scalar.copy)
+        group_x(last, 1, share, 512, nc.vector.tensor_copy)
+        affine(last - 2, gain, ALU.mult, nc.vector, 2, 4)
+        quantize_x(last, 1)
+        square(last - 1, 0)
+        square(last - 1, 1)
         sum_squares(last - 1)
+        capsules(last, range(1, 2))
+        centre_gained(last - 1, 1)
         inverse_root(last - 1)
-        subtract_mean(last)
+        affine(last - 2, shift, ALU.add, nc.vector)
+        store(last - 2)
+        centre_plain(last)
+        centre_gained(last, 0)
+        centre_gained(last, 1)
         normalise(last - 1, 0)
         normalise(last - 1, 1)
-        steps = [(2 * q, 2 * q + len(rows)) for q, rows in enumerate(pairs(last))]
-        for q in range(len(steps)):
-            square(last, q)
-        affine(last - 1, gain, ALU.mult, nc.vector)
-        for q, (lo, hi) in enumerate(steps):
-            sum_squares(last, lo, hi)
-            inverse_root(last, lo, hi)
-            if q == 0:
-                affine(last - 1, shift, ALU.add, nc.vector)
-                store(last - 1)
-        for q in range(len(steps)):
-            normalise(last, q)
-        for lo, hi in steps:
-            affine(last, gain, ALU.mult, nc.vector, lo, hi)
-        for lo, hi in steps:
-            affine(last, shift, ALU.add, nc.vector, lo, hi)
-            store(last, lo, hi)
+        square(last, 0)
+        square(last, 1)
+        affine(last - 1, shift, ALU.add, nc.vector, 0, 2)
+        sum_squares(last, 0, 2)
+        inverse_root(last, 0, 2)
+        affine(last - 1, shift, ALU.add, nc.vector, 2, 4)
+        store(last - 1)
+        sum_squares(last, 2, 4)
+        inverse_root(last, 2, 4)
+        normalise(last, 0)
+        normalise(last, 1)
+        for lo in (0, 2):
+            affine(last, shift, ALU.add, nc.vector, lo, lo + 2)
+            store(last, lo, lo + 2)

@@ -22,404 +22,396 @@ P = 128
 PACK = 4
 K_PASS = P * PACK
 PASSES = H1 // K_PASS
-GROUP_ROWS = [4] * 8
-GROUPS = len(GROUP_ROWS)
-ON_TENSOR = range(5)
-SCALAR_SHARE = [0,0,384,384,384,384,0,128]
+BANK = 512
+GROUP = 512
+ROWS = GROUP // P
+PAIRS = ROWS // 2
+GROUPS = TOKENS // GROUP
+LAST = GROUPS - 1
+HALVES = OUT // P
+RUN = 4
+
+STEADY_SHARE = 384
+LAST_SHARE = 128
+SUMS_ON_TENSOR = range(LAST - 2)
+GAIN_ON_TENSOR = range(LAST - 1, GROUPS)
 
 
 def tile_capsulenetwork_pa_t_kernel(tc, h1_bytes, h1_scale, W2, b2, Wp, bp, ln_g, ln_b, out):
     nc = tc.nc
-    first = [P * sum(GROUP_ROWS[:i]) for i in range(GROUPS + 1)]
-    out_rows = [out[first[i]:first[i + 1]].rearrange("(p j) n d -> p (j n d)", p=P) for i in range(GROUPS)]
-    h1_rows = [h1_bytes[first[i]:first[i + 1]].rearrange("(p j) k -> p (j k)", p=P) for i in range(GROUPS)]
+    h1_pairs = h1_bytes.rearrange("(i p q j) k -> i q p (j k)", p=P, q=PAIRS, j=2)
+    out_rows = out.rearrange("(i p j) n d -> i p (j n d)", p=P, j=ROWS)
+    w2_parts = W2.rearrange("(g p t) (G c) -> G g p t c", p=P, t=PACK, c=K_PASS)
+    wp_parts = Wp.rearrange("n (G p t) d -> G p n (t d)", p=P, t=PACK)
 
     with ExitStack() as ctx:
         keep = ctx.enter_context(tc.tile_pool(name="keep", bufs=1))
         work = ctx.enter_context(tc.tile_pool(name="work", bufs=2))
         banks = ctx.enter_context(tc.psum_pool(name="banks", bufs=6))
-        centred_banks = ctx.enter_context(tc.psum_pool(name="centred_banks", bufs=2))
+        centred_banks = ctx.enter_context(tc.psum_pool(name="centred_banks", bufs=PAIRS))
         ctx.enter_context(tc.manual_schedule())
 
-        scale_cols = keep.tile([P, H1 // P], F32, name="scale_cols")
-        nc.sync.dma_start(out=scale_cols[:], in_=h1_scale.rearrange("o (p c) -> p (o c)", p=P))
-        w2_view = W2.rearrange("(g p j) (G c) -> G g p j c", p=P, j=PACK, c=K_PASS)
-        w2_raw = {}
-        h1_raw = {}
+        h1_raw, w2_raw, wp_raw = {}, {}, {}
+
+        def load_h1(i, q):
+            h1_raw[i, q] = keep.tile([P, 2 * H1], U8, name="h1_raw%d%d" % (i, q))
+            nc.sync.dma_start(out=h1_raw[i, q][:], in_=h1_pairs[i, q])
 
         def load_w2(G, g):
             w2_raw[G, g] = keep.tile([P, PACK, K_PASS], BF16, name="w2_raw%d%d" % (G, g))
-            nc.sync.dma_start(out=w2_raw[G, g][:], in_=w2_view[G, g])
+            nc.sync.dma_start(out=w2_raw[G, g][:], in_=w2_parts[G, g])
 
-        def load_h1(i):
-            h1_raw[i] = keep.tile([P, GROUP_ROWS[i] * H1], U8, name="h1_raw%d" % i)
-            nc.sync.dma_start(out=h1_raw[i][:], in_=h1_rows[i])
-
+        scale_cols = keep.tile([P, PASSES, PACK], F32, name="scale_cols")
+        nc.sync.dma_start(out=scale_cols[:], in_=h1_scale.rearrange("o (g p t) -> p (o g) t", p=P, t=PACK))
+        load_h1(0, 0)
         load_w2(0, 0)
-        load_h1(0)
+        load_h1(0, 1)
         load_w2(0, 1)
         load_w2(1, 0)
         load_w2(1, 1)
-        load_h1(1)
-        b2_cols = keep.tile([P, PASSES, PACK], BF16, name="b2_cols")
-        nc.sync.dma_start(out=b2_cols[:], in_=b2.rearrange("(G p t) -> p G t", p=P, t=PACK))
-        load_h1(2)
-        wp_raw = {}
-        wp_view = Wp.rearrange("n (G p j) d -> G p n (j d)", p=P, j=PACK)
-        for G in range(PASSES):
-            wp_raw[G] = keep.tile([P, CAPS, PACK * DIM], BF16, name="wp_raw%d" % G)
-            nc.sync.dma_start(out=wp_raw[G][:], in_=wp_view[G])
-        bp_cols = keep.tile([P, 2, 2], BF16, name="bp_cols")
-        with nc.allow_non_contiguous_dma(reason="one bias value to a partition"):
-            nc.sync.dma_start(out=bp_cols[:, :, 0:1], in_=bp.rearrange("(h n) (d o) -> (n d) h o", h=2, o=1))
-        gain = keep.tile([P, OUT], BF16, name="gain")
-        nc.sync.dma_start(out=gain[:], in_=ln_g.rearrange("n d -> (n d)").partition_broadcast(P))
-        shift = keep.tile([P, OUT], BF16, name="shift")
-        nc.sync.dma_start(out=shift[:], in_=ln_b.rearrange("n d -> (n d)").partition_broadcast(P))
-        for i in range(3, GROUPS):
-            load_h1(i)
 
         ident = keep.tile([P, P], F32, name="ident")
         make_identity(nc, ident[:])
         centre = keep.tile([P, P], F32, name="centre")
-        blocks = [[-DIM, P // DIM], [0, DIM]]
+        capsule_start = [[-DIM, P // DIM], [0, DIM]]
         nc.gpsimd.memset(centre[:], 0.0)
         nc.gpsimd.affine_select(out=centre[:], in_=centre[:], compare_op=ALU.is_gt, fill=-1.0 / DIM,
-                                base=1 - DIM, pattern=blocks, channel_multiplier=1)
+                                base=1 - DIM, pattern=capsule_start, channel_multiplier=1)
         nc.gpsimd.affine_select(out=centre[:], in_=centre[:], compare_op=ALU.is_ge, fill=0.0,
-                                base=0, pattern=blocks, channel_multiplier=1)
+                                base=0, pattern=capsule_start, channel_multiplier=1)
         nc.gpsimd.affine_select(out=centre[:], in_=centre[:], compare_op=ALU.not_equal, fill=1.0 - 1.0 / DIM,
                                 base=0, pattern=[[-1, P]], channel_multiplier=1)
 
         warm = keep.tile([P, 1], F32, name="warm")
         nc.scalar.activation(out=warm[:], in_=ident[:, 0:1], func=ACT.Abs_reciprocal_sqrt, bias=LN_EPS, scale=1.0)
 
-        scale_all = keep.tile([P, H1], F32, name="scale_all")
-        per_bank = 4
-        for half in range(2):
-            bank = banks.tile([P, 512], F32, name="bank")
-            for c in range(per_bank):
-                col = half * per_bank + c
-                nc.tensor.transpose(bank[:, c * P:(c + 1) * P], scale_cols[:, col:col + 1].to_broadcast([P, P]), ident[:])
-            nc.scalar.copy(out=scale_all[:].rearrange("q (p c) -> q p c", c=H1 // P)[:, :, half * per_bank:(half + 1) * per_bank],
-                           in_=bank[:].rearrange("q (c p) -> q p c", c=per_bank))
+        scale_all = keep.tile([P, 2 * H1], F32, name="scale_all")
+        for g, copy in enumerate((nc.vector.tensor_copy, nc.scalar.copy)):
+            bank = banks.tile([P, BANK], F32, name="bank")
+            for t in range(PACK):
+                nc.tensor.transpose(bank[:, t * P:(t + 1) * P], scale_cols[:, g, t:t + 1].to_broadcast([P, P]), ident[:])
+            copy(out=scale_all[:, g * K_PASS:(g + 1) * K_PASS].rearrange("r (p t) -> r p t", t=PACK),
+                 in_=bank[:].rearrange("r (t p) -> r p t", t=PACK))
+        nc.sync.dma_start(out=scale_all[:, H1:2 * H1], in_=scale_all[:, 0:H1])
+
+        load_h1(1, 0)
+        load_h1(1, 1)
+        b2_cols = keep.tile([P, PASSES, PACK], BF16, name="b2_cols")
+        nc.sync.dma_start(out=b2_cols[:], in_=b2.rearrange("(G p t) -> p G t", p=P, t=PACK))
+        load_h1(2, 0)
+        load_h1(2, 1)
+        for G in range(PASSES):
+            wp_raw[G] = keep.tile([P, CAPS, PACK * DIM], BF16, name="wp_raw%d" % G)
+            nc.sync.dma_start(out=wp_raw[G][:], in_=wp_parts[G])
+        bp_cols = keep.tile([P, HALVES, 2], BF16, name="bp_cols")
+        with nc.allow_non_contiguous_dma(reason="one bias value to a partition"):
+            nc.sync.dma_start(out=bp_cols[:, :, 0:1], in_=bp.rearrange("(h n) (d o) -> (n d) h o", h=HALVES, o=1))
+        gain = keep.tile([P, OUT], BF16, name="gain")
+        nc.sync.dma_start(out=gain[:], in_=ln_g.rearrange("n d -> (n d)").partition_broadcast(P))
+        shift = keep.tile([P, OUT], BF16, name="shift")
+        nc.sync.dma_start(out=shift[:], in_=ln_b.rearrange("n d -> (n d)").partition_broadcast(P))
+        for i in range(3, GROUPS):
+            for q in range(PAIRS):
+                load_h1(i, q)
 
         w2_codes = keep.tile([P, PASSES, H2], U32, name="w2_codes", align_bytes=64)
         w2_scales = keep.tile([P, PASSES, H2], U8, name="w2_scales", align_bytes=64)
         wp_codes = keep.tile([P, PASSES, OUT], U32, name="wp_codes", align_bytes=64)
         wp_scales = keep.tile([P, PASSES, OUT], U8, name="wp_scales", align_bytes=64)
-        w2_grouped = {}
-        wp_grouped = {}
+        centre_gain = keep.tile([P, HALVES, P], F32, name="centre_gain")
+        w2_grouped, wp_grouped = {}, {}
+
+        def quantize(codes, scales, grouped):
+            nc.vector.quantize_mx(out=codes.bitcast(FP8X4), scales=scales, in_=grouped)
 
         def group_w2(G, g, copy):
             w2_grouped[G, g] = keep.tile([P, K_PASS * PACK], BF16, name="w2_grouped%d%d" % (G, g), align_bytes=64)
-            copy(out=w2_grouped[G, g][:].rearrange("p (t m j) -> p m t j", t=PACK, j=PACK),
-                 in_=w2_raw[G, g][:].rearrange("p j (m t) -> p m t j", t=PACK))
+            copy(out=w2_grouped[G, g][:].rearrange("p (s m t) -> p m s t", s=PACK, t=PACK),
+                 in_=w2_raw[G, g][:].rearrange("p t (m s) -> p m s t", s=PACK))
 
         def quantize_w2(G, g):
             cols = slice(G * K_PASS, (G + 1) * K_PASS)
-            nc.vector.quantize_mx(out=w2_codes[:, g, cols].bitcast(FP8X4), scales=w2_scales[:, g, cols], in_=w2_grouped[G, g][:])
+            quantize(w2_codes[:, g, cols], w2_scales[:, g, cols], w2_grouped[G, g][:])
 
         def group_wp(G):
             wp_grouped[G] = keep.tile([P, OUT * PACK], BF16, name="wp_grouped%d" % G, align_bytes=64)
-            nc.scalar.copy(out=wp_grouped[G][:].rearrange("p (n d j) -> p n d j", d=DIM, j=PACK),
-                           in_=wp_raw[G][:].rearrange("p n (j d) -> p n d j", j=PACK))
+            nc.scalar.copy(out=wp_grouped[G][:].rearrange("p (n d t) -> p n d t", d=DIM, t=PACK),
+                           in_=wp_raw[G][:].rearrange("p n (t d) -> p n d t", t=PACK))
 
         def quantize_wp(G):
-            nc.vector.quantize_mx(out=wp_codes[:, G, :].bitcast(FP8X4), scales=wp_scales[:, G, :], in_=wp_grouped[G][:])
+            quantize(wp_codes[:, G, :], wp_scales[:, G, :], wp_grouped[G][:])
+
+        def fold_gain():
+            nc.vector.tensor_tensor(out=centre_gain[:], in0=centre[:].unsqueeze(1).to_broadcast([P, HALVES, P]),
+                                    in1=gain[:].rearrange("p (h c) -> p h c", h=HALVES), op=ALU.mult)
 
         h1_wide, h1_grouped, h1_codes, h1_scales = {}, {}, {}, {}
         x_planes, x_grouped, x_codes, x_scales = {}, {}, {}, {}
-        u_cols, centred, squares, sums, rstd, result = {}, {}, {}, {}, {}, {}
-
-        sum_bank = {}
-        capsule_bank = {}
+        u_bank, u_cols, centred, gained, squares, sums, rstd, result = {}, {}, {}, {}, {}, {}, {}, {}
 
         def valid(i):
             return 0 <= i < GROUPS
 
-        def pairs(i):
-            rows = GROUP_ROWS[i] if valid(i) else 0
-            return [range(lo, min(lo + 2, rows)) for lo in range(0, rows, 2)]
+        def widen(i, q, lo=0, hi=2):
+            if lo == 0:
+                h1_wide[i, q] = work.tile([P, 2 * H1], BF16, name="h1_wide", bufs=6)
+            nc.vector.tensor_tensor(out=h1_wide[i, q][:, lo * H1:hi * H1], in0=h1_raw[i, q][:, lo * H1:hi * H1].bitcast(FP8),
+                                    in1=scale_all[:, 0:(hi - lo) * H1], op=ALU.mult)
 
-        def widen(i, pair):
-            if pair >= len(pairs(i)):
-                return
-            for j in pairs(i)[pair]:
-                h1_wide[i, j] = work.tile([P, H1], BF16, name="h1_wide", bufs=12, align_bytes=64)
-                nc.vector.tensor_tensor(out=h1_wide[i, j][:], in0=h1_raw[i][:, j * H1:(j + 1) * H1].bitcast(FP8),
-                                        in1=scale_all[:], op=ALU.mult)
-
-        def turn(i, pair):
-            for rows in pairs(i)[pair:pair + 1]:
-                width = len(rows) * P
+        def turn(i):
+            words_pass = K_PASS // 2
+            for q in range(PAIRS):
+                words = h1_wide[i, q][:].bitcast(F32).rearrange("p (j w) -> p j w", j=2)
                 for g in range(PASSES):
-                    if pair == 0:
-                        h1_grouped[i, g] = work.tile([P, GROUP_ROWS[i] * P * PACK], BF16, name="h1_grouped", bufs=4, align_bytes=64)
-                    words_out = h1_grouped[i, g][:].bitcast(F32).rearrange("p (n u) -> p n u", u=2)
-                    bank = banks.tile([P, 512], F32, name="bank")
+                    if q == 0:
+                        h1_grouped[i, g] = work.tile([P, GROUP * PACK], BF16, name="h1_grouped", bufs=4, align_bytes=64)
+                    bank = banks.tile([P, BANK], F32, name="bank")
                     for u in range(2):
-                        for jj, j in enumerate(rows):
-                            words = h1_wide[i, j][:].bitcast(F32)
-                            col = u * width + jj * P
-                            nc.tensor.transpose(bank[:, col:col + P], words[:, 256 * g + u:256 * (g + 1):2], ident[:])
-                    nc.scalar.copy(out=words_out[:, 256 * pair:256 * pair + width, :],
-                                   in_=bank[:, 0:2 * width].rearrange("p (u n) -> p n u", u=2))
+                        for j in range(2):
+                            col = (2 * u + j) * P
+                            nc.tensor.transpose(bank[:, col:col + P],
+                                                words[:, j, words_pass * g + u:words_pass * (g + 1):2], ident[:])
+                    grouped_words = h1_grouped[i, g][:].bitcast(F32).rearrange("p (n u) -> p n u", u=2)
+                    nc.scalar.copy(out=grouped_words[:, 2 * P * q:2 * P * (q + 1), :],
+                                   in_=bank[:].rearrange("p (u n) -> p n u", u=2))
 
-        def quantize_h1(i, g):
-            if not valid(i):
-                return
-            n = GROUP_ROWS[i] * P
-            h1_codes[i, g] = work.tile([P, n], U32, name="h1_codes", bufs=4, align_bytes=64)
-            h1_scales[i, g] = work.tile([P, n], U8, name="h1_scales", bufs=4, align_bytes=64)
-            nc.vector.quantize_mx(out=h1_codes[i, g][:].bitcast(FP8X4), scales=h1_scales[i, g][:], in_=h1_grouped[i, g][:])
+        def quantize_h1(i):
+            for g in range(PASSES):
+                h1_codes[i, g] = work.tile([P, GROUP], U32, name="h1_codes", bufs=4, align_bytes=64)
+                h1_scales[i, g] = work.tile([P, GROUP], U8, name="h1_scales", bufs=4, align_bytes=64)
+                quantize(h1_codes[i, g][:], h1_scales[i, g][:], h1_grouped[i, g][:])
 
-        def hidden(i, G, planes):
-            if not valid(i):
-                return
-            n = GROUP_ROWS[i] * P
-            for t in planes:
-                if t == 0:
-                    x_planes[i, G] = work.tile([P, PACK, n], BF16, name="x_planes", bufs=4)
-                bank = banks.tile([P, 512], F32, name="bank")
-                cols = slice((G * PACK + t) * P, (G * PACK + t + 1) * P)
+        def hidden(i, G, slices):
+            for s in slices:
+                if s == 0:
+                    x_planes[i, G] = work.tile([P, PACK, GROUP], BF16, name="x_planes", bufs=4)
+                bank = banks.tile([P, BANK], F32, name="bank")
+                cols = slice(G * K_PASS + s * P, G * K_PASS + (s + 1) * P)
                 for g in range(PASSES):
-                    nc.tensor.matmul_mx(out=bank[:, 0:n], lhsT=w2_codes[:, g, cols].bitcast(FP8X4), lhsT_scale=w2_scales[:, g, cols],
+                    nc.tensor.matmul_mx(out=bank[:], lhsT=w2_codes[:, g, cols].bitcast(FP8X4), lhsT_scale=w2_scales[:, g, cols],
                                         rhs=h1_codes[i, g][:].bitcast(FP8X4), rhs_scale=h1_scales[i, g][:],
                                         start=(g == 0), stop=(g == PASSES - 1))
-                nc.scalar.activation(out=x_planes[i, G][:, t, :], in_=bank[:, 0:n], func=ACT.Relu, bias=b2_cols[:, G, t:t + 1], scale=1.0)
+                nc.scalar.activation(out=x_planes[i, G][:, s, :], in_=bank[:], func=ACT.Relu, bias=b2_cols[:, G, s:s + 1], scale=1.0)
 
         def group_x(i, G, lo, hi, copy):
-            if not valid(i) or lo >= hi:
+            if lo == hi:
                 return
             if (i, G) not in x_grouped:
-                x_grouped[i, G] = work.tile([P, GROUP_ROWS[i] * P * PACK], BF16, name="x_grouped", bufs=4, align_bytes=64)
-            dst = x_grouped[i, G][:].rearrange("p (c n t) -> p c t n", n=4, t=PACK)
-            src = x_planes[i, G][:].rearrange("p t (c n) -> p c t n", n=4)
-            copy(out=dst[:, lo // 4:hi // 4], in_=src[:, lo // 4:hi // 4])
+                x_grouped[i, G] = work.tile([P, GROUP * PACK], BF16, name="x_grouped", bufs=4, align_bytes=64)
+            dst = x_grouped[i, G][:].rearrange("p (c n t) -> p c t n", n=RUN, t=PACK)
+            src = x_planes[i, G][:].rearrange("p t (c n) -> p c t n", n=RUN)
+            copy(out=dst[:, lo // RUN:hi // RUN], in_=src[:, lo // RUN:hi // RUN])
 
         def quantize_x(i, G):
             if not valid(i):
                 return
-            n = GROUP_ROWS[i] * P
-            x_codes[i, G] = work.tile([P, n], U32, name="x_codes", bufs=4, align_bytes=64)
-            x_scales[i, G] = work.tile([P, n], U8, name="x_scales", bufs=4, align_bytes=64)
-            nc.vector.quantize_mx(out=x_codes[i, G][:].bitcast(FP8X4), scales=x_scales[i, G][:], in_=x_grouped[i, G][:])
+            x_codes[i, G] = work.tile([P, GROUP], U32, name="x_codes", bufs=4, align_bytes=64)
+            x_scales[i, G] = work.tile([P, GROUP], U8, name="x_scales", bufs=4, align_bytes=64)
+            quantize(x_codes[i, G][:], x_scales[i, G][:], x_grouped[i, G][:])
 
         def capsules(i, passes=range(PASSES)):
             if not valid(i):
                 return
-            for h in range(2):
+            for h in range(HALVES):
                 cols = slice(h * P, (h + 1) * P)
                 for G in passes:
                     if G == 0:
-                        capsule_bank[i, h] = banks.tile([P, 512], F32, name="bank")
-                    nc.tensor.matmul_mx(out=capsule_bank[i, h][:], lhsT=wp_codes[:, G, cols].bitcast(FP8X4), lhsT_scale=wp_scales[:, G, cols],
+                        u_bank[i, h] = banks.tile([P, BANK], F32, name="bank")
+                    nc.tensor.matmul_mx(out=u_bank[i, h][:], lhsT=wp_codes[:, G, cols].bitcast(FP8X4), lhsT_scale=wp_scales[:, G, cols],
                                         rhs=x_codes[i, G][:].bitcast(FP8X4), rhs_scale=x_scales[i, G][:],
                                         start=(G == 0), stop=(G == PASSES - 1))
                 if PASSES - 1 in passes:
-                    u_cols[i, h] = work.tile([P, 512], F32, name="u_cols", bufs=4)
-                    nc.scalar.activation(out=u_cols[i, h][:], in_=capsule_bank[i, h][:], func=ACT.Identity, bias=bp_cols[:, h, 0:1], scale=1.0)
+                    u_cols[i, h] = work.tile([P, GROUP], F32, name="u_cols", bufs=4)
+                    nc.scalar.activation(out=u_cols[i, h][:], in_=u_bank[i, h][:], func=ACT.Identity, bias=bp_cols[:, h, 0:1], scale=1.0)
 
-        def subtract_mean(i, which, matrices, pool, name):
-            for pair in (which if valid(i) else ()):
-                rows = pairs(i)[pair]
-                bank = pool.tile([P, 512], F32, name=name)
-                for jj, j in enumerate(rows):
-                    for h in range(2):
-                        col = jj * OUT + h * P
-                        nc.tensor.matmul(bank[:, col:col + P], lhsT=u_cols[i, h][:, j * P:(j + 1) * P], rhs=matrices[h],
-                                         start=True, stop=True)
-                centred[i, pair, name] = bank
+        def times_matrix(i, q, bank, matrices):
+            for j in range(2):
+                tokens = slice((2 * q + j) * P, (2 * q + j + 1) * P)
+                for h in range(HALVES):
+                    col = j * OUT + h * P
+                    nc.tensor.matmul(bank[:, col:col + P], lhsT=u_cols[i, h][:, tokens], rhs=matrices[h], start=True, stop=True)
 
-        centre_gain = keep.tile([P, 2, P], F32, name="centre_gain")
-
-        def fold_gain():
-            nc.vector.tensor_tensor(out=centre_gain[:], in0=centre[:].unsqueeze(1).to_broadcast([P, 2, P]),
-                                    in1=gain[:].rearrange("p (h c) -> p h c", h=2), op=ALU.mult)
-
-        def centre_plain(i):
-            subtract_mean(i, range(2), [centre[:], centre[:]], centred_banks, "centred")
-
-        def centre_gained(i, pair):
-            subtract_mean(i, [pair], [centre_gain[:, 0, :], centre_gain[:, 1, :]], banks, "bank")
-
-        def square(i, pair):
-            if pair >= len(pairs(i)):
+        def subtract_mean(i):
+            if not valid(i):
                 return
-            if pair == 0:
-                squares[i] = work.tile([P, GROUP_ROWS[i] * OUT], F32, name="squares")
-            width = len(pairs(i)[pair]) * OUT
-            if i in ON_TENSOR:
-                nc.scalar.activation(out=squares[i][:].rearrange("p (d c) -> p d c", d=DIM)[:, :, 64 * pair:64 * (pair + 1)],
-                                     in_=centred[i, pair, "centred"][:].rearrange("p (c d) -> p d c", d=DIM), func=ACT.Square)
+            for q in range(PAIRS):
+                centred[i, q] = centred_banks.tile([P, BANK], F32, name="centred")
+                times_matrix(i, q, centred[i, q], [centre[:]] * HALVES)
+
+        def subtract_mean_with_gain(i, q):
+            gained[i, q] = banks.tile([P, BANK], F32, name="bank")
+            times_matrix(i, q, gained[i, q], [centre_gain[:, h, :] for h in range(HALVES)])
+
+        def square(i, q):
+            if not valid(i):
+                return
+            if q == 0:
+                squares[i] = work.tile([P, ROWS * OUT], F32, name="squares")
+            if i in SUMS_ON_TENSOR:
+                dst = squares[i][:].rearrange("p (d c) -> p d c", d=DIM)[:, :, 2 * CAPS * q:2 * CAPS * (q + 1)]
+                src = centred[i, q][:].rearrange("p (c d) -> p d c", d=DIM)
             else:
-                nc.scalar.activation(out=squares[i][:, 512 * pair:512 * pair + width], in_=centred[i, pair, "centred"][:, 0:width], func=ACT.Square)
+                dst = squares[i][:, BANK * q:BANK * (q + 1)]
+                src = centred[i, q][:]
+            nc.scalar.activation(out=dst, in_=src, func=ACT.Square)
 
-        def add_squares(i):
-            if i not in ON_TENSOR:
+        def inverse_root(dst, src):
+            nc.scalar.activation(out=dst, in_=src, func=ACT.Abs_reciprocal_sqrt, bias=LN_EPS, scale=1.0 / DIM)
+
+        def add_squares_on_tensor(i):
+            if not valid(i):
                 return
-            sum_bank[i] = banks.tile([P, 512], F32, name="bank")
+            bank = banks.tile([P, BANK], F32, name="bank")
             for d in range(DIM):
-                nc.tensor.matmul(sum_bank[i][:, 0:P], lhsT=squares[i][:, d * P:(d + 1) * P], rhs=ident[:],
+                nc.tensor.matmul(bank[:, 0:P], lhsT=squares[i][:, d * P:(d + 1) * P], rhs=ident[:],
                                  start=(d == 0), stop=(d == DIM - 1), is_transpose=True)
             sums[i] = work.tile([P, P], F32, name="sums")
-            nc.scalar.copy(out=sums[i][:], in_=sum_bank[i][:, 0:P])
+            nc.scalar.copy(out=sums[i][:], in_=bank[:, 0:P])
 
-        def turn_sums_back(i):
-            if i not in ON_TENSOR:
+        def roots_from_turned_sums(i):
+            if not valid(i):
                 return
-            bank = banks.tile([P, 512], F32, name="bank")
+            bank = banks.tile([P, BANK], F32, name="bank")
             nc.tensor.transpose(bank[:, 0:P], sums[i][:], ident[:])
-            rstd[i] = work.tile([P, P], F32, name="rstd")
-            nc.scalar.activation(out=rstd[i][:], in_=bank[:, 0:P], func=ACT.Abs_reciprocal_sqrt, bias=LN_EPS, scale=1.0 / DIM)
+            rstd[i] = work.tile([P, ROWS * CAPS], F32, name="rstd")
+            inverse_root(rstd[i][:], bank[:, 0:P])
 
-        def sum_squares(i, lo=0, hi=None):
-            if not valid(i) or i in ON_TENSOR:
-                return
-            hi = GROUP_ROWS[i] if hi is None else hi
+        def add_squares_on_vector(i, lo, hi):
             if lo == 0:
-                sums[i] = work.tile([P, GROUP_ROWS[i] * CAPS], F32, name="sums")
+                sums[i] = work.tile([P, ROWS * CAPS], F32, name="sums")
             nc.vector.tensor_reduce(out=sums[i][:, lo * CAPS:hi * CAPS],
-                                    in_=squares[i][:, lo * OUT:hi * OUT].rearrange("p (n d) -> p n d", d=DIM), axis=AXIS.X, op=ALU.add)
+                                    in_=squares[i][:, lo * OUT:hi * OUT].rearrange("p (c d) -> p c d", d=DIM), axis=AXIS.X, op=ALU.add)
 
-        def inverse_root(i, lo=0, hi=None):
-            if not valid(i) or i in ON_TENSOR:
-                return
-            hi = GROUP_ROWS[i] if hi is None else hi
+        def roots_from_sums(i, lo, hi):
             if lo == 0:
-                rstd[i] = work.tile([P, GROUP_ROWS[i] * CAPS], F32, name="rstd")
-            nc.scalar.activation(out=rstd[i][:, lo * CAPS:hi * CAPS], in_=sums[i][:, lo * CAPS:hi * CAPS],
-                                 func=ACT.Abs_reciprocal_sqrt, bias=LN_EPS, scale=1.0 / DIM)
+                rstd[i] = work.tile([P, ROWS * CAPS], F32, name="rstd")
+            inverse_root(rstd[i][:, lo * CAPS:hi * CAPS], sums[i][:, lo * CAPS:hi * CAPS])
 
-        def normalise(i, pair):
-            for rows in pairs(i)[pair:pair + 1]:
-                if pair == 0:
-                    result[i] = work.tile([P, GROUP_ROWS[i] * OUT], F32, name="result", bufs=3)
-                caps = len(rows) * CAPS
-                nc.vector.tensor_tensor(out=result[i][:, 512 * pair:512 * pair + caps * DIM].rearrange("p (n d) -> p n d", d=DIM),
-                                        in0=centred[i, pair, "bank" if i >= GROUPS - 2 else "centred"][:, 0:caps * DIM].rearrange("p (n d) -> p n d", d=DIM),
-                                        in1=rstd[i][:, 64 * pair:64 * pair + caps].unsqueeze(2).to_broadcast([P, caps, DIM]),
-                                        op=ALU.mult)
-
-        def affine(i, vector, op, engine, lo=0, hi=None):
+        def normalise(i):
             if not valid(i):
                 return
-            hi = GROUP_ROWS[i] if hi is None else hi
+            result[i] = work.tile([P, ROWS * OUT], F32, name="result", bufs=3)
+            source = gained if i in GAIN_ON_TENSOR else centred
+            for q in range(PAIRS):
+                factors = rstd[i][:, 2 * CAPS * q:2 * CAPS * (q + 1)].unsqueeze(2).to_broadcast([P, 2 * CAPS, DIM])
+                nc.vector.tensor_tensor(out=result[i][:, BANK * q:BANK * (q + 1)].rearrange("p (c d) -> p c d", d=DIM),
+                                        in0=source[i, q][:].rearrange("p (c d) -> p c d", d=DIM), in1=factors, op=ALU.mult)
+
+        def per_channel(i, vector, op, lo, hi):
             rows = result[i][:].rearrange("p (j c) -> p j c", c=OUT)[:, lo:hi, :]
-            engine.tensor_tensor(out=rows, in0=rows, in1=vector[:].unsqueeze(1).to_broadcast([P, hi - lo, OUT]), op=op)
+            nc.vector.tensor_tensor(out=rows, in0=rows, in1=vector[:].unsqueeze(1).to_broadcast([P, hi - lo, OUT]), op=op)
 
-        def store(i, lo=0, hi=None):
-            if not valid(i):
-                return
-            hi = GROUP_ROWS[i] if hi is None else hi
-            nc.sync.dma_start(out=out_rows[i][:, lo * OUT:hi * OUT], in_=result[i][:, lo * OUT:hi * OUT])
+        def apply_gain(i, lo=0, hi=ROWS):
+            if valid(i):
+                per_channel(i, gain, ALU.mult, lo, hi)
 
-        group_w2(0, 0, nc.vector.tensor_copy)
-        widen(0, 0)
+        def apply_shift(i, lo=0, hi=ROWS):
+            if valid(i):
+                per_channel(i, shift, ALU.add, lo, hi)
+
+        def store(i, lo=0, hi=ROWS):
+            if valid(i):
+                nc.sync.dma_start(out=out_rows[i][:, lo * OUT:hi * OUT], in_=result[i][:, lo * OUT:hi * OUT])
+
+        widen(0, 0, 0, 1)
+        widen(0, 0, 1, 2)
+        group_w2(0, 0, nc.scalar.copy)
+        widen(0, 1, 0, 1)
+        widen(0, 1, 1, 2)
         group_w2(0, 1, nc.scalar.copy)
+        turn(0)
         quantize_w2(0, 0)
-        widen(0, 1)
-        turn(0, 0)
-        turn(0, 1)
-        quantize_w2(0, 1)
         group_w2(1, 0, nc.vector.tensor_copy)
-        group_w2(1, 1, nc.scalar.copy)
-        quantize_h1(0, 0)
-        quantize_h1(0, 1)
+        quantize_w2(0, 1)
         quantize_w2(1, 0)
-        widen(1, 0)
+        group_w2(1, 1, nc.scalar.copy)
+        quantize_h1(0)
+        widen(1, 0, 0, 1)
         quantize_w2(1, 1)
-        last = GROUPS - 1
-        for k in range(last):
-            share = SCALAR_SHARE[k]
+        widen(1, 0, 1, 2)
+
+        for k in range(LAST):
+            share = STEADY_SHARE if valid(k - 2) and valid(k + 2) else 0
             quantize_x(k - 1, 1)
             if k == 1:
                 quantize_wp(0)
                 quantize_wp(1)
-            hidden(k, 0, range(4))
+            hidden(k, 0, range(PACK))
             widen(k + 1, 1)
             hidden(k, 1, range(0, 2))
-            add_squares(k - 2)
-            hidden(k, 1, range(2, 4))
-            turn_sums_back(k - 2)
+            add_squares_on_tensor(k - 2)
+            hidden(k, 1, range(2, PACK))
+            roots_from_turned_sums(k - 2)
             if k == 2:
                 fold_gain()
             capsules(k - 1)
-            group_x(k, 0, 0, 512, nc.vector.tensor_copy)
-            normalise(k - 2, 0)
-            normalise(k - 2, 1)
-            turn(k + 1, 0)
-            turn(k + 1, 1)
+            group_x(k, 0, 0, GROUP, nc.vector.tensor_copy)
+            normalise(k - 2)
+            turn(k + 1)
             if k == 0:
                 group_wp(0)
                 group_wp(1)
-            group_x(k, 1, share, 512, nc.vector.tensor_copy)
+            group_x(k, 1, share, GROUP, nc.vector.tensor_copy)
             quantize_x(k, 0)
-            if k == last - 1:
+            if k == LAST - 1:
                 break
-            affine(k - 2, gain, ALU.mult, nc.vector)
-            quantize_h1(k + 1, 0)
-            quantize_h1(k + 1, 1)
-            centre_plain(k - 1)
+            apply_gain(k - 2)
+            quantize_h1(k + 1)
+            subtract_mean(k - 1)
             group_x(k, 1, 0, share // 2, nc.scalar.copy)
             square(k - 1, 0)
             group_x(k, 1, share // 2, share, nc.scalar.copy)
             square(k - 1, 1)
-            affine(k - 2, shift, ALU.add, nc.vector)
+            apply_shift(k - 2)
             store(k - 2)
             widen(k + 2, 0)
-        share = SCALAR_SHARE[last]
-        quantize_h1(last, 0)
-        quantize_h1(last, 1)
-        quantize_x(last - 1, 1)
-        centre_plain(last - 2)
-        square(last - 2, 0)
-        square(last - 2, 1)
-        affine(last - 3, gain, ALU.mult, nc.vector)
-        sum_squares(last - 2)
-        affine(last - 3, shift, ALU.add, nc.vector)
-        store(last - 3)
-        hidden(last, 0, range(4))
-        inverse_root(last - 2)
-        capsules(last - 1)
-        hidden(last, 1, range(4))
-        normalise(last - 2, 0)
-        normalise(last - 2, 1)
-        group_x(last, 0, 0, 512, nc.vector.tensor_copy)
-        affine(last - 2, gain, ALU.mult, nc.vector, 0, 2)
-        quantize_x(last, 0)
-        centre_plain(last - 1)
-        centre_gained(last - 1, 0)
-        capsules(last, range(1))
-        group_x(last, 1, 0, share, nc.scalar.copy)
-        group_x(last, 1, share, 512, nc.vector.tensor_copy)
-        affine(last - 2, gain, ALU.mult, nc.vector, 2, 4)
-        quantize_x(last, 1)
-        square(last - 1, 0)
-        square(last - 1, 1)
-        sum_squares(last - 1)
-        capsules(last, range(1, 2))
-        centre_gained(last - 1, 1)
-        inverse_root(last - 1)
-        affine(last - 2, shift, ALU.add, nc.vector)
-        store(last - 2)
-        centre_plain(last)
-        centre_gained(last, 0)
-        centre_gained(last, 1)
-        normalise(last - 1, 0)
-        normalise(last - 1, 1)
-        square(last, 0)
-        square(last, 1)
-        affine(last - 1, shift, ALU.add, nc.vector, 0, 2)
-        sum_squares(last, 0, 2)
-        inverse_root(last, 0, 2)
-        affine(last - 1, shift, ALU.add, nc.vector, 2, 4)
-        store(last - 1)
-        sum_squares(last, 2, 4)
-        inverse_root(last, 2, 4)
-        normalise(last, 0)
-        normalise(last, 1)
-        for lo in (0, 2):
-            affine(last, shift, ALU.add, nc.vector, lo, lo + 2)
-            store(last, lo, lo + 2)
+
+        quantize_h1(LAST)
+        quantize_x(LAST - 1, 1)
+        subtract_mean(LAST - 2)
+        square(LAST - 2, 0)
+        square(LAST - 2, 1)
+        apply_gain(LAST - 3)
+        add_squares_on_vector(LAST - 2, 0, ROWS)
+        apply_shift(LAST - 3)
+        store(LAST - 3)
+
+        hidden(LAST, 0, range(PACK))
+        roots_from_sums(LAST - 2, 0, ROWS)
+        capsules(LAST - 1)
+        hidden(LAST, 1, range(PACK))
+        normalise(LAST - 2)
+        group_x(LAST, 0, 0, GROUP, nc.vector.tensor_copy)
+        apply_gain(LAST - 2, 0, 2)
+        quantize_x(LAST, 0)
+        subtract_mean(LAST - 1)
+        subtract_mean_with_gain(LAST - 1, 0)
+        capsules(LAST, range(0, 1))
+        group_x(LAST, 1, 0, LAST_SHARE, nc.scalar.copy)
+        group_x(LAST, 1, LAST_SHARE, GROUP, nc.vector.tensor_copy)
+        apply_gain(LAST - 2, 2, ROWS)
+        quantize_x(LAST, 1)
+        square(LAST - 1, 0)
+        square(LAST - 1, 1)
+        add_squares_on_vector(LAST - 1, 0, ROWS)
+        capsules(LAST, range(1, PASSES))
+        subtract_mean_with_gain(LAST - 1, 1)
+        roots_from_sums(LAST - 1, 0, ROWS)
+        apply_shift(LAST - 2)
+        store(LAST - 2)
+
+        subtract_mean(LAST)
+        for q in range(PAIRS):
+            subtract_mean_with_gain(LAST, q)
+        normalise(LAST - 1)
+        for q in range(PAIRS):
+            square(LAST, q)
+        for q in range(PAIRS):
+            apply_shift(LAST - 1, 2 * q, 2 * q + 2)
+            add_squares_on_vector(LAST, 2 * q, 2 * q + 2)
+            roots_from_sums(LAST, 2 * q, 2 * q + 2)
+        store(LAST - 1)
+        normalise(LAST)
+        for q in range(PAIRS):
+            apply_shift(LAST, 2 * q, 2 * q + 2)
+            store(LAST, 2 * q, 2 * q + 2)

from contextlib import ExitStack

import concourse.mybir as mybir
from concourse.masks import make_identity

F32 = mybir.dt.float32
BF16 = mybir.dt.bfloat16
U32 = mybir.dt.uint32
U8 = mybir.dt.uint8
FP8 = mybir.dt.float8_e4m3fn
FP8X4 = mybir.dt.float8_e4m3fn_x4
ALU = mybir.AluOpType
ACT = mybir.ActivationFunctionType
AXIS = mybir.AxisListType

TOKENS, H1, H2, CAPS, DIM = 4096, 1024, 1024, 32, 8
OUT = CAPS * DIM
LN_EPS = 1e-5
FLOPS = 2 * TOKENS * H1 * H2 + 2 * TOKENS * H2 * OUT

P = 128
PACK = 4
K_PASS = P * PACK
PASSES = H1 // K_PASS
BANK = 512
GROUP = 512
ROWS = GROUP // P
PAIRS = ROWS // 2
GROUPS = TOKENS // GROUP
LAST = GROUPS - 1
HALVES = OUT // P
RUN = 4

STEADY_SHARE = 384
LAST_SHARE = 128
SUMS_ON_TENSOR = range(LAST - 2)
GAIN_ON_TENSOR = range(LAST - 1, GROUPS)


def tile_capsulenetwork_pa_t_kernel(tc, h1_bytes, h1_scale, W2, b2, Wp, bp, ln_g, ln_b, out):
    nc = tc.nc
    h1_pairs = h1_bytes.rearrange("(i p q j) k -> i q p (j k)", p=P, q=PAIRS, j=2)
    out_rows = out.rearrange("(i p j) n d -> i p (j n d)", p=P, j=ROWS)
    w2_parts = W2.rearrange("(g p t) (G c) -> G g p t c", p=P, t=PACK, c=K_PASS)
    wp_parts = Wp.rearrange("n (G p t) d -> G p n (t d)", p=P, t=PACK)

    with ExitStack() as ctx:
        keep = ctx.enter_context(tc.tile_pool(name="keep", bufs=1))
        work = ctx.enter_context(tc.tile_pool(name="work", bufs=2))
        banks = ctx.enter_context(tc.psum_pool(name="banks", bufs=6))
        centred_banks = ctx.enter_context(tc.psum_pool(name="centred_banks", bufs=PAIRS))
        ctx.enter_context(tc.manual_schedule())

        h1_raw, w2_raw, wp_raw = {}, {}, {}

        def load_h1(i, q):
            h1_raw[i, q] = keep.tile([P, 2 * H1], U8, name="h1_raw%d%d" % (i, q))
            nc.sync.dma_start(out=h1_raw[i, q][:], in_=h1_pairs[i, q])

        def load_w2(G, g):
            w2_raw[G, g] = keep.tile([P, PACK, K_PASS], BF16, name="w2_raw%d%d" % (G, g))
            nc.sync.dma_start(out=w2_raw[G, g][:], in_=w2_parts[G, g])

        scale_cols = keep.tile([P, PASSES, PACK], F32, name="scale_cols")
        nc.sync.dma_start(out=scale_cols[:], in_=h1_scale.rearrange("o (g p t) -> p (o g) t", p=P, t=PACK))
        load_h1(0, 0)
        load_w2(0, 0)
        load_h1(0, 1)
        load_w2(0, 1)
        load_w2(1, 0)
        load_w2(1, 1)

        ident = keep.tile([P, P], F32, name="ident")
        make_identity(nc, ident[:])
        centre = keep.tile([P, P], F32, name="centre")
        capsule_start = [[-DIM, P // DIM], [0, DIM]]
        nc.gpsimd.memset(centre[:], 0.0)
        nc.gpsimd.affine_select(out=centre[:], in_=centre[:], compare_op=ALU.is_gt, fill=-1.0 / DIM,
                                base=1 - DIM, pattern=capsule_start, channel_multiplier=1)
        nc.gpsimd.affine_select(out=centre[:], in_=centre[:], compare_op=ALU.is_ge, fill=0.0,
                                base=0, pattern=capsule_start, channel_multiplier=1)
        nc.gpsimd.affine_select(out=centre[:], in_=centre[:], compare_op=ALU.not_equal, fill=1.0 - 1.0 / DIM,
                                base=0, pattern=[[-1, P]], channel_multiplier=1)

        warm = keep.tile([P, 1], F32, name="warm")
        nc.scalar.activation(out=warm[:], in_=ident[:, 0:1], func=ACT.Abs_reciprocal_sqrt, bias=LN_EPS, scale=1.0)

        scale_all = keep.tile([P, 2 * H1], F32, name="scale_all")
        for g, copy in enumerate((nc.vector.tensor_copy, nc.scalar.copy)):
            bank = banks.tile([P, BANK], F32, name="bank")
            for t in range(PACK):
                nc.tensor.transpose(bank[:, t * P:(t + 1) * P], scale_cols[:, g, t:t + 1].to_broadcast([P, P]), ident[:])
            copy(out=scale_all[:, g * K_PASS:(g + 1) * K_PASS].rearrange("r (p t) -> r p t", t=PACK),
                 in_=bank[:].rearrange("r (t p) -> r p t", t=PACK))
        nc.sync.dma_start(out=scale_all[:, H1:2 * H1], in_=scale_all[:, 0:H1])

        load_h1(1, 0)
        load_h1(1, 1)
        b2_cols = keep.tile([P, PASSES, PACK], BF16, name="b2_cols")
        nc.sync.dma_start(out=b2_cols[:], in_=b2.rearrange("(G p t) -> p G t", p=P, t=PACK))
        load_h1(2, 0)
        load_h1(2, 1)
        for G in range(PASSES):
            wp_raw[G] = keep.tile([P, CAPS, PACK * DIM], BF16, name="wp_raw%d" % G)
            nc.sync.dma_start(out=wp_raw[G][:], in_=wp_parts[G])
        bp_cols = keep.tile([P, HALVES, 2], BF16, name="bp_cols")
        with nc.allow_non_contiguous_dma(reason="one bias value to a partition"):
            nc.sync.dma_start(out=bp_cols[:, :, 0:1], in_=bp.rearrange("(h n) (d o) -> (n d) h o", h=HALVES, o=1))
        gain = keep.tile([P, OUT], BF16, name="gain")
        nc.sync.dma_start(out=gain[:], in_=ln_g.rearrange("n d -> (n d)").partition_broadcast(P))
        shift = keep.tile([P, OUT], BF16, name="shift")
        nc.sync.dma_start(out=shift[:], in_=ln_b.rearrange("n d -> (n d)").partition_broadcast(P))
        for i in range(3, GROUPS):
            for q in range(PAIRS):
                load_h1(i, q)

        w2_codes = keep.tile([P, PASSES, H2], U32, name="w2_codes", align_bytes=64)
        w2_scales = keep.tile([P, PASSES, H2], U8, name="w2_scales", align_bytes=64)
        wp_codes = keep.tile([P, PASSES, OUT], U32, name="wp_codes", align_bytes=64)
        wp_scales = keep.tile([P, PASSES, OUT], U8, name="wp_scales", align_bytes=64)
        centre_gain = keep.tile([P, HALVES, P], F32, name="centre_gain")
        w2_grouped, wp_grouped = {}, {}

        def quantize(codes, scales, grouped):
            nc.vector.quantize_mx(out=codes.bitcast(FP8X4), scales=scales, in_=grouped)

        def group_w2(G, g, copy):
            w2_grouped[G, g] = keep.tile([P, K_PASS * PACK], BF16, name="w2_grouped%d%d" % (G, g), align_bytes=64)
            copy(out=w2_grouped[G, g][:].rearrange("p (s m t) -> p m s t", s=PACK, t=PACK),
                 in_=w2_raw[G, g][:].rearrange("p t (m s) -> p m s t", s=PACK))

        def quantize_w2(G, g):
            cols = slice(G * K_PASS, (G + 1) * K_PASS)
            quantize(w2_codes[:, g, cols], w2_scales[:, g, cols], w2_grouped[G, g][:])

        def group_wp(G):
            wp_grouped[G] = keep.tile([P, OUT * PACK], BF16, name="wp_grouped%d" % G, align_bytes=64)
            nc.scalar.copy(out=wp_grouped[G][:].rearrange("p (n d t) -> p n d t", d=DIM, t=PACK),
                           in_=wp_raw[G][:].rearrange("p n (t d) -> p n d t", t=PACK))

        def quantize_wp(G):
            quantize(wp_codes[:, G, :], wp_scales[:, G, :], wp_grouped[G][:])

        def fold_gain():
            nc.vector.tensor_tensor(out=centre_gain[:], in0=centre[:].unsqueeze(1).to_broadcast([P, HALVES, P]),
                                    in1=gain[:].rearrange("p (h c) -> p h c", h=HALVES), op=ALU.mult)

        h1_wide, h1_grouped, h1_codes, h1_scales = {}, {}, {}, {}
        x_planes, x_grouped, x_codes, x_scales = {}, {}, {}, {}
        u_bank, u_cols, centred, gained, squares, sums, rstd, result = {}, {}, {}, {}, {}, {}, {}, {}

        def valid(i):
            return 0 <= i < GROUPS

        def widen(i, q, lo=0, hi=2):
            if lo == 0:
                h1_wide[i, q] = work.tile([P, 2 * H1], BF16, name="h1_wide", bufs=6)
            nc.vector.tensor_tensor(out=h1_wide[i, q][:, lo * H1:hi * H1], in0=h1_raw[i, q][:, lo * H1:hi * H1].bitcast(FP8),
                                    in1=scale_all[:, 0:(hi - lo) * H1], op=ALU.mult)

        def turn(i):
            words_pass = K_PASS // 2
            for q in range(PAIRS):
                words = h1_wide[i, q][:].bitcast(F32).rearrange("p (j w) -> p j w", j=2)
                for g in range(PASSES):
                    if q == 0:
                        h1_grouped[i, g] = work.tile([P, GROUP * PACK], BF16, name="h1_grouped", bufs=4, align_bytes=64)
                    bank = banks.tile([P, BANK], F32, name="bank")
                    for u in range(2):
                        for j in range(2):
                            col = (2 * u + j) * P
                            nc.tensor.transpose(bank[:, col:col + P],
                                                words[:, j, words_pass * g + u:words_pass * (g + 1):2], ident[:])
                    grouped_words = h1_grouped[i, g][:].bitcast(F32).rearrange("p (n u) -> p n u", u=2)
                    nc.scalar.copy(out=grouped_words[:, 2 * P * q:2 * P * (q + 1), :],
                                   in_=bank[:].rearrange("p (u n) -> p n u", u=2))

        def quantize_h1(i):
            for g in range(PASSES):
                h1_codes[i, g] = work.tile([P, GROUP], U32, name="h1_codes", bufs=4, align_bytes=64)
                h1_scales[i, g] = work.tile([P, GROUP], U8, name="h1_scales", bufs=4, align_bytes=64)
                quantize(h1_codes[i, g][:], h1_scales[i, g][:], h1_grouped[i, g][:])

        def hidden(i, G, slices):
            for s in slices:
                if s == 0:
                    x_planes[i, G] = work.tile([P, PACK, GROUP], BF16, name="x_planes", bufs=4)
                bank = banks.tile([P, BANK], F32, name="bank")
                cols = slice(G * K_PASS + s * P, G * K_PASS + (s + 1) * P)
                for g in range(PASSES):
                    nc.tensor.matmul_mx(out=bank[:], lhsT=w2_codes[:, g, cols].bitcast(FP8X4), lhsT_scale=w2_scales[:, g, cols],
                                        rhs=h1_codes[i, g][:].bitcast(FP8X4), rhs_scale=h1_scales[i, g][:],
                                        start=(g == 0), stop=(g == PASSES - 1))
                nc.scalar.activation(out=x_planes[i, G][:, s, :], in_=bank[:], func=ACT.Relu, bias=b2_cols[:, G, s:s + 1], scale=1.0)

        def group_x(i, G, lo, hi, copy):
            if lo == hi:
                return
            if (i, G) not in x_grouped:
                x_grouped[i, G] = work.tile([P, GROUP * PACK], BF16, name="x_grouped", bufs=4, align_bytes=64)
            dst = x_grouped[i, G][:].rearrange("p (c n t) -> p c t n", n=RUN, t=PACK)
            src = x_planes[i, G][:].rearrange("p t (c n) -> p c t n", n=RUN)
            copy(out=dst[:, lo // RUN:hi // RUN], in_=src[:, lo // RUN:hi // RUN])

        def quantize_x(i, G):
            if not valid(i):
                return
            x_codes[i, G] = work.tile([P, GROUP], U32, name="x_codes", bufs=4, align_bytes=64)
            x_scales[i, G] = work.tile([P, GROUP], U8, name="x_scales", bufs=4, align_bytes=64)
            quantize(x_codes[i, G][:], x_scales[i, G][:], x_grouped[i, G][:])

        def capsules(i, passes=range(PASSES)):
            if not valid(i):
                return
            for h in range(HALVES):
                cols = slice(h * P, (h + 1) * P)
                for G in passes:
                    if G == 0:
                        u_bank[i, h] = banks.tile([P, BANK], F32, name="bank")
                    nc.tensor.matmul_mx(out=u_bank[i, h][:], lhsT=wp_codes[:, G, cols].bitcast(FP8X4), lhsT_scale=wp_scales[:, G, cols],
                                        rhs=x_codes[i, G][:].bitcast(FP8X4), rhs_scale=x_scales[i, G][:],
                                        start=(G == 0), stop=(G == PASSES - 1))
                if PASSES - 1 in passes:
                    u_cols[i, h] = work.tile([P, GROUP], F32, name="u_cols", bufs=4)
                    nc.scalar.activation(out=u_cols[i, h][:], in_=u_bank[i, h][:], func=ACT.Identity, bias=bp_cols[:, h, 0:1], scale=1.0)

        def times_matrix(i, q, bank, matrices):
            for j in range(2):
                tokens = slice((2 * q + j) * P, (2 * q + j + 1) * P)
                for h in range(HALVES):
                    col = j * OUT + h * P
                    nc.tensor.matmul(bank[:, col:col + P], lhsT=u_cols[i, h][:, tokens], rhs=matrices[h], start=True, stop=True)

        def subtract_mean(i):
            if not valid(i):
                return
            for q in range(PAIRS):
                centred[i, q] = centred_banks.tile([P, BANK], F32, name="centred")
                times_matrix(i, q, centred[i, q], [centre[:]] * HALVES)

        def subtract_mean_with_gain(i, q):
            gained[i, q] = banks.tile([P, BANK], F32, name="bank")
            times_matrix(i, q, gained[i, q], [centre_gain[:, h, :] for h in range(HALVES)])

        def square(i, q):
            if not valid(i):
                return
            if q == 0:
                squares[i] = work.tile([P, ROWS * OUT], F32, name="squares")
            if i in SUMS_ON_TENSOR:
                dst = squares[i][:].rearrange("p (d c) -> p d c", d=DIM)[:, :, 2 * CAPS * q:2 * CAPS * (q + 1)]
                src = centred[i, q][:].rearrange("p (c d) -> p d c", d=DIM)
            else:
                dst = squares[i][:, BANK * q:BANK * (q + 1)]
                src = centred[i, q][:]
            nc.scalar.activation(out=dst, in_=src, func=ACT.Square)

        def inverse_root(dst, src):
            nc.scalar.activation(out=dst, in_=src, func=ACT.Abs_reciprocal_sqrt, bias=LN_EPS, scale=1.0 / DIM)

        def add_squares_on_tensor(i):
            if not valid(i):
                return
            bank = banks.tile([P, BANK], F32, name="bank")
            for d in range(DIM):
                nc.tensor.matmul(bank[:, 0:P], lhsT=squares[i][:, d * P:(d + 1) * P], rhs=ident[:],
                                 start=(d == 0), stop=(d == DIM - 1), is_transpose=True)
            sums[i] = work.tile([P, P], F32, name="sums")
            nc.scalar.copy(out=sums[i][:], in_=bank[:, 0:P])

        def roots_from_turned_sums(i):
            if not valid(i):
                return
            bank = banks.tile([P, BANK], F32, name="bank")
            nc.tensor.transpose(bank[:, 0:P], sums[i][:], ident[:])
            rstd[i] = work.tile([P, ROWS * CAPS], F32, name="rstd")
            inverse_root(rstd[i][:], bank[:, 0:P])

        def add_squares_on_vector(i, lo, hi):
            if lo == 0:
                sums[i] = work.tile([P, ROWS * CAPS], F32, name="sums")
            nc.vector.tensor_reduce(out=sums[i][:, lo * CAPS:hi * CAPS],
                                    in_=squares[i][:, lo * OUT:hi * OUT].rearrange("p (c d) -> p c d", d=DIM), axis=AXIS.X, op=ALU.add)

        def roots_from_sums(i, lo, hi):
            if lo == 0:
                rstd[i] = work.tile([P, ROWS * CAPS], F32, name="rstd")
            inverse_root(rstd[i][:, lo * CAPS:hi * CAPS], sums[i][:, lo * CAPS:hi * CAPS])

        def normalise(i):
            if not valid(i):
                return
            result[i] = work.tile([P, ROWS * OUT], F32, name="result", bufs=3)
            source = gained if i in GAIN_ON_TENSOR else centred
            for q in range(PAIRS):
                factors = rstd[i][:, 2 * CAPS * q:2 * CAPS * (q + 1)].unsqueeze(2).to_broadcast([P, 2 * CAPS, DIM])
                nc.vector.tensor_tensor(out=result[i][:, BANK * q:BANK * (q + 1)].rearrange("p (c d) -> p c d", d=DIM),
                                        in0=source[i, q][:].rearrange("p (c d) -> p c d", d=DIM), in1=factors, op=ALU.mult)

        def per_channel(i, vector, op, lo, hi):
            rows = result[i][:].rearrange("p (j c) -> p j c", c=OUT)[:, lo:hi, :]
            nc.vector.tensor_tensor(out=rows, in0=rows, in1=vector[:].unsqueeze(1).to_broadcast([P, hi - lo, OUT]), op=op)

        def apply_gain(i, lo=0, hi=ROWS):
            if valid(i):
                per_channel(i, gain, ALU.mult, lo, hi)

        def apply_shift(i, lo=0, hi=ROWS):
            if valid(i):
                per_channel(i, shift, ALU.add, lo, hi)

        def store(i, lo=0, hi=ROWS):
            if valid(i):
                nc.sync.dma_start(out=out_rows[i][:, lo * OUT:hi * OUT], in_=result[i][:, lo * OUT:hi * OUT])

        widen(0, 0, 0, 1)
        widen(0, 0, 1, 2)
        group_w2(0, 0, nc.scalar.copy)
        widen(0, 1, 0, 1)
        widen(0, 1, 1, 2)
        group_w2(0, 1, nc.scalar.copy)
        turn(0)
        quantize_w2(0, 0)
        group_w2(1, 0, nc.vector.tensor_copy)
        quantize_w2(0, 1)
        quantize_w2(1, 0)
        group_w2(1, 1, nc.scalar.copy)
        quantize_h1(0)
        widen(1, 0, 0, 1)
        quantize_w2(1, 1)
        widen(1, 0, 1, 2)

        for k in range(LAST):
            share = STEADY_SHARE if valid(k - 2) and valid(k + 2) else 0
            quantize_x(k - 1, 1)
            if k == 1:
                quantize_wp(0)
                quantize_wp(1)
            hidden(k, 0, range(PACK))
            widen(k + 1, 1)
            hidden(k, 1, range(0, 2))
            add_squares_on_tensor(k - 2)
            hidden(k, 1, range(2, PACK))
            roots_from_turned_sums(k - 2)
            if k == 2:
                fold_gain()
            capsules(k - 1)
            group_x(k, 0, 0, GROUP, nc.vector.tensor_copy)
            normalise(k - 2)
            turn(k + 1)
            if k == 0:
                group_wp(0)
                group_wp(1)
            group_x(k, 1, share, GROUP, nc.vector.tensor_copy)
            quantize_x(k, 0)
            if k == LAST - 1:
                break
            apply_gain(k - 2)
            quantize_h1(k + 1)
            subtract_mean(k - 1)
            group_x(k, 1, 0, share // 2, nc.scalar.copy)
            square(k - 1, 0)
            group_x(k, 1, share // 2, share, nc.scalar.copy)
            square(k - 1, 1)
            apply_shift(k - 2)
            store(k - 2)
            widen(k + 2, 0)

        quantize_h1(LAST)
        quantize_x(LAST - 1, 1)
        subtract_mean(LAST - 2)
        square(LAST - 2, 0)
        square(LAST - 2, 1)
        apply_gain(LAST - 3)
        add_squares_on_vector(LAST - 2, 0, ROWS)
        apply_shift(LAST - 3)
        store(LAST - 3)

        hidden(LAST, 0, range(PACK))
        roots_from_sums(LAST - 2, 0, ROWS)
        capsules(LAST - 1)
        hidden(LAST, 1, range(PACK))
        normalise(LAST - 2)
        group_x(LAST, 0, 0, GROUP, nc.vector.tensor_copy)
        apply_gain(LAST - 2, 0, 2)
        quantize_x(LAST, 0)
        subtract_mean(LAST - 1)
        subtract_mean_with_gain(LAST - 1, 0)
        capsules(LAST, range(0, 1))
        group_x(LAST, 1, 0, LAST_SHARE, nc.scalar.copy)
        group_x(LAST, 1, LAST_SHARE, GROUP, nc.vector.tensor_copy)
        apply_gain(LAST - 2, 2, ROWS)
        quantize_x(LAST, 1)
        square(LAST - 1, 0)
        square(LAST - 1, 1)
        add_squares_on_vector(LAST - 1, 0, ROWS)
        capsules(LAST, range(1, PASSES))
        subtract_mean_with_gain(LAST - 1, 1)
        roots_from_sums(LAST - 1, 0, ROWS)
        apply_shift(LAST - 2)
        store(LAST - 2)

        subtract_mean(LAST)
        for q in range(PAIRS):
            subtract_mean_with_gain(LAST, q)
        normalise(LAST - 1)
        for q in range(PAIRS):
            square(LAST, q)
        for q in range(PAIRS):
            apply_shift(LAST - 1, 2 * q, 2 * q + 2)
            add_squares_on_vector(LAST, 2 * q, 2 * q + 2)
            roots_from_sums(LAST, 2 * q, 2 * q + 2)
        store(LAST - 1)
        normalise(LAST)
        for q in range(PAIRS):
            apply_shift(LAST, 2 * q, 2 * q + 2)
            store(LAST, 2 * q, 2 * q + 2)
